import numpy as np
import ml_dtypes


def mxq(x, axis, fmt="e4m3"):
    dtype, down = {"e4m3": (ml_dtypes.float8_e4m3fn, 7), "e5m2": (ml_dtypes.float8_e5m2, 14)}[fmt]
    v = np.moveaxis(np.asarray(x, np.float32).astype(ml_dtypes.bfloat16).astype(np.float64), axis, -1)
    blocks = v.reshape(v.shape[:-1] + (-1, 32))
    amax = np.abs(blocks).max(-1, keepdims=True)
    byte = np.maximum(np.where(amax > 0, np.frexp(amax)[1] - 1 + 127, 0) - down, 1)
    scale = np.exp2(byte - 127.0)
    codes = (blocks / scale).astype(np.float32).astype(dtype).astype(np.float64)
    return np.moveaxis((codes * scale).reshape(v.shape), -1, axis)


BF16 = ml_dtypes.bfloat16


def bf(x):
    return np.asarray(x, np.float32).astype(BF16)


def f64(x):
    return np.asarray(x).astype(np.float64)


S, B, D, N = 2, 2, 1024, 1024
EPS = 1e-10
N_ITERS = 20
TEMP = 1.0


def logsumexp(a, axis):
    m = a.max(axis=axis, keepdims=True)
    return m + np.log(np.exp(a - m).sum(axis=axis, keepdims=True))


def sinkhorn(log_alpha, temp, n_iters):
    la = log_alpha / temp
    for _ in range(n_iters):
        la = la - logsumexp(la, -2)
        la = la - logsumexp(la, -1)
    return np.exp(la)


def setup_inputs():
    return {"x": bf(np.random.standard_normal((B, D, N)) * np.sqrt(N) / 8.0),
            "log_alpha": bf(np.random.uniform(-2.0, 2.0, (N, N))),
            "u": bf(0.004 + 0.988 * np.random.random_sample((S, B, N, N)))}


def reference(x, log_alpha, u):
    gumbel = -np.log(EPS - np.log(f64(u) + EPS))
    log_alpha_noise = f64(log_alpha) + gumbel
    soft_perms = sinkhorn(log_alpha_noise, TEMP, N_ITERS)
    return mxq(f64(x), 2, "e4m3")[None] @ mxq(soft_perms, 2, "e4m3")

from contextlib import ExitStack

import concourse.mybir as mybir
from concourse.masks import make_identity

F32 = mybir.dt.float32
BF16 = mybir.dt.bfloat16
U32 = mybir.dt.uint32
U8 = mybir.dt.uint8
FP8X4 = mybir.dt.float8_e4m3fn_x4
ALU = mybir.AluOpType
AF = mybir.ActivationFunctionType
AX = mybir.AxisListType

S, B, D, N = 2, 2, 1024, 1024
P = 128
NB = N // P
HALF = 512
EPS = 1e-10
ROUNDS = 20
FLOPS = 2 * S * B * D * N * N
MANUAL = False


def tile_sinkhornpermutation_kernel(tc, x, log_alpha, u, out):
    nc = tc.nc
    with ExitStack() as ctx:
        if MANUAL:
            ctx.enter_context(tc.manual_schedule())
        const = ctx.enter_context(tc.tile_pool(name="const", bufs=1))
        psum = ctx.enter_context(tc.psum_pool(name="psum", bufs=1))

        ident = const.tile([P, P], F32, name="ident")
        make_identity(nc, ident[:])
        la = const.tile([P, NB, N], BF16, name="la")
        xc = const.tile([P, B, 2, D], U32, name="xc", align_bytes=64)
        xs = const.tile([P, B, 2, D], U8, name="xs", align_bytes=64)
        scr = const.tile([P, HALF], F32, name="scr")
        pmax = const.tile([P, 1], F32, name="pmax")
        gmax = const.tile([P, 1], F32, name="gmax")
        negmax = const.tile([P, 1], F32, name="negmax")

        kf = [const.tile([P, NB, N], F32, name="kf%d" % s) for s in range(2)]
        k1 = [const.tile([P, NB, N], BF16, name="k1%d" % s) for s in range(2)]
        k2 = [const.tile([P, NB, N], BF16, name="k2%d" % s) for s in range(2)]
        rs = [const.tile([P, NB, 2], BF16, name="rs%d" % s) for s in range(2)]
        acc = [const.tile([P, NB, 2], F32, name="acc%d" % s) for s in range(2)]
        rsum = [const.tile([P, NB], F32, name="rsum%d" % s) for s in range(2)]
        r = [const.tile([P, NB], F32, name="r%d" % s) for s in range(2)]
        csum = [const.tile([P, NB], F32, name="csum%d" % s) for s in range(2)]
        c = [const.tile([P, NB], F32, name="c%d" % s) for s in range(2)]
        cs = [psum.tile([P, NB, 2], F32, name="cs%d" % s) for s in range(2)]
        cb = [[psum.tile([P, HALF], F32, name="cb%d%d" % (s, h)) for h in range(2)] for s in range(2)]

        upool = ctx.enter_context(tc.tile_pool(name="upool", bufs=1))

        def load_u(q):
            si, bi = divmod(q, B)
            ut = upool.tile([P, NB, N], BF16, name="ut", tag="ut")
            for g in range(2):
                nc.sync.dma_start(
                    out=ut[:, 4 * g : 4 * g + 4, :],
                    in_=u[si, bi, HALF * g : HALF * (g + 1), :].rearrange("(p t) m -> p t m", t=4),
                )
            return ut

        def setup(s, q, ut):
            eng = nc.vector if q == 0 else nc.gpsimd
            for i in range(NB):
                nc.scalar.activation(out=kf[s][:, i, :], in_=ut[:, i, :], func=AF.Ln, bias=EPS, scale=1.0)
                nc.scalar.activation(out=kf[s][:, i, :], in_=kf[s][:, i, :], func=AF.Ln, bias=EPS, scale=-1.0)
                eng.tensor_tensor(out=kf[s][:, i, :], in0=la[:, i, :], in1=kf[s][:, i, :], op=ALU.subtract)
            for i in range(NB):
                nc.scalar.activation(out=kf[s][:, i, :], in_=kf[s][:, i, :], func=AF.Exp, bias=negmax[:, 0:1], scale=1.0)
                if q == 0:
                    nc.vector.tensor_copy(out=k1[s][:, i, :], in_=kf[s][:, i, :])
                else:
                    nc.scalar.copy(out=k1[s][:, i, :], in_=kf[s][:, i, :])
                eng.tensor_tensor(out=k2[s][:, i, :], in0=kf[s][:, i, :], in1=k1[s][:, i, :], op=ALU.subtract)
            nc.vector.memset(rs[s][:, :, 0:1], 1.0)
            nc.vector.memset(rs[s][:, :, 1:2], 0.0)

        def colsum(s, lo, hi):
            for i in range(lo, hi):
                for j in range(NB):
                    cols = slice(j * P, (j + 1) * P)
                    nc.tensor.matmul(
                        out=cs[s][:, j, 0:2], lhsT=k1[s][:, i, cols], rhs=rs[s][:, i, 0:2],
                        start=(i == 0 and j == 0), stop=False,
                    )
                    nc.tensor.matmul(
                        out=cs[s][:, j, 0:1], lhsT=k2[s][:, i, cols], rhs=rs[s][:, i, 0:1],
                        start=False, stop=(i == NB - 1 and j == NB - 1),
                    )

        def c_chain(s):
            nc.vector.tensor_reduce(out=csum[s][:], in_=cs[s][:], axis=AX.X, op=ALU.add)
            nc.vector.reciprocal(out=c[s][:], in_=csum[s][:])
            for j in range(NB):
                nc.tensor.transpose(
                    out=cb[s][j // 4][:, (j % 4) * P : (j % 4 + 1) * P],
                    in_=c[s][:, j : j + 1].to_broadcast([P, P]),
                    identity=ident[:],
                )

        def half(s, lo, hi, last):
            for i in range(lo, hi):
                for h in range(2):
                    nc.vector.scalar_tensor_tensor(
                        out=scr[:], in0=kf[s][:, i, HALF * h : HALF * (h + 1)], scalar=1.0, in1=cb[s][h][:],
                        op0=ALU.mult, op1=ALU.mult, accum_out=acc[s][:, i, h : h + 1],
                    )
            nc.vector.tensor_reduce(out=rsum[s][:, lo:hi], in_=acc[s][:, lo:hi, :], axis=AX.X, op=ALU.add)
            nc.vector.reciprocal(out=r[s][:, lo:hi], in_=rsum[s][:, lo:hi])
            if not last:
                nc.vector.tensor_copy(out=rs[s][:, lo:hi, 0:1], in_=r[s][:, lo:hi].unsqueeze(2))
                nc.vector.tensor_tensor(
                    out=rs[s][:, lo:hi, 1:2], in0=r[s][:, lo:hi].unsqueeze(2), in1=rs[s][:, lo:hi, 0:1], op=ALU.subtract
                )
                colsum(s, lo, hi)

        def prep_x():
            with tc.tile_pool(name="xprep", bufs=1) as xp:
                for b in range(B):
                    gx = [xp.tile([P, D, 2], F32, name="gx%d" % g, tag="gx%d" % g, align_bytes=64) for g in range(2)]
                    for db in range(D // P):
                        xr = xp.tile([P, N], BF16, name="xr", tag="xr", bufs=4)
                        nc.sync.dma_start(out=xr[:], in_=x[b, db * P : (db + 1) * P, :])
                        xw = xr[:].bitcast(F32)
                        xt = psum.tile([P, 4, P], F32, name="mm", tag="mm", bufs=2)
                        for g in range(2):
                            for w in range(2):
                                nc.tensor.transpose(
                                    out=xt[:, 2 * g + w, :], in_=xw[:, 256 * g + w : 256 * (g + 1) : 2], identity=ident[:]
                                )
                        for g in range(2):
                            nc.vector.tensor_copy(
                                out=gx[g][:, db * P : (db + 1) * P, :],
                                in_=xt[:, 2 * g : 2 * g + 2, :].rearrange("p w d -> p d w"),
                            )
                    for g in range(2):
                        nc.vector.quantize_mx(
                            out=xc[:, b, g, :].bitcast(FP8X4),
                            scales=xs[:, b, g, :],
                            in_=gx[g][:].rearrange("p d w -> p (d w)").bitcast(BF16),
                        )

        def final(fin, s, q):
            si, bi = divmod(q, B)
            for i in range(NB):
                nc.scalar.activation(out=kf[s][:, i, :], in_=kf[s][:, i, :], func=AF.Copy, scale=r[s][:, i : i + 1])
            pc = fin.tile([P, 2, N], U32, name="pc", tag="pc", align_bytes=64)
            ps = fin.tile([P, 2, N], U8, name="ps", tag="ps", align_bytes=64)
            for g in range(2):
                grp = fin.tile([P, N, 4], BF16, name="grp", tag="grp", bufs=2, align_bytes=64)
                for h in range(2):
                    nc.vector.tensor_tensor(
                        out=grp[:, HALF * h : HALF * (h + 1), :],
                        in0=kf[s][:, 4 * g : 4 * g + 4, HALF * h : HALF * (h + 1)].rearrange("p t m -> p m t"),
                        in1=cb[s][h][:].unsqueeze(2).to_broadcast([P, HALF, 4]),
                        op=ALU.mult,
                    )
                nc.vector.quantize_mx(
                    out=pc[:, g, :].bitcast(FP8X4), scales=ps[:, g, :], in_=grp[:].rearrange("p m t -> p (m t)")
                )
            for db in range(D // P):
                ost = fin.tile([P, N], F32, name="ost", tag="ost", bufs=3)
                rows = slice(db * P, (db + 1) * P)
                for h in range(2):
                    cols = slice(HALF * h, HALF * (h + 1))
                    mm = psum.tile([P, HALF], F32, name="mm", tag="mm", bufs=2)
                    for g in range(2):
                        nc.tensor.matmul_mx(
                            out=mm[:],
                            lhsT=xc[:, bi, g, rows].bitcast(FP8X4), lhsT_scale=xs[:, bi, g, rows],
                            rhs=pc[:, g, cols].bitcast(FP8X4), rhs_scale=ps[:, g, cols],
                            start=(g == 0), stop=(g == 1),
                        )
                    nc.scalar.copy(out=ost[:, cols], in_=mm[:])
                nc.sync.dma_start(out=out[si, bi, rows, :], in_=ost[:])

        ut0 = load_u(0)
        for g in range(2):
            nc.sync.dma_start(
                out=la[:, 4 * g : 4 * g + 4, :],
                in_=log_alpha[HALF * g : HALF * (g + 1), :].rearrange("(p t) m -> p t m", t=4),
            )
        nc.vector.tensor_reduce(out=pmax[:], in_=la[:].rearrange("p i m -> p (i m)"), axis=AX.X, op=ALU.max)
        mt = psum.tile([P, P], F32, name="mm", tag="mm", bufs=2)
        nc.tensor.transpose(out=mt[:], in_=pmax[:, 0:1].to_broadcast([P, P]), identity=ident[:])
        nc.vector.tensor_reduce(out=gmax[:], in_=mt[:], axis=AX.X, op=ALU.max)
        nc.vector.tensor_scalar_mul(out=negmax[:], in0=gmax[:], scalar1=-1.0)

        setup(0, 0, ut0)
        colsum(0, 0, NB)
        setup(1, 1, load_u(1))
        colsum(1, 0, NB)
        prep_x()
        fin = ctx.enter_context(tc.tile_pool(name="fin", bufs=1))

        def start(s, q):
            setup(s, q, load_u(q))
            colsum(s, 0, NB)

        def life(s, q, with_start):
            segs = []
            if with_start:
                segs.append(("S", lambda: start(s, q)))
            for k in range(ROUNDS):
                segs.append(("A", lambda: c_chain(s)))
                segs.append(("B", lambda last=(k == ROUNDS - 1): half(s, 0, 4, last)))
                segs.append(("C", lambda last=(k == ROUNDS - 1): half(s, 4, NB, last)))
            segs.append(("F", lambda: final(fin, s, q)))
            return segs

        todo = [life(0, 0, False) + life(0, 2, True), life(1, 1, False) + life(1, 3, True)]
        pos = [0, 0]

        def emit(s, kind):
            if pos[s] < len(todo[s]) and todo[s][pos[s]][0] == kind:
                todo[s][pos[s]][1]()
                pos[s] += 1

        def advance_to_a(s):
            while pos[s] < len(todo[s]) and todo[s][pos[s]][0] not in ("B", "C"):
                kind = todo[s][pos[s]][0]
                todo[s][pos[s]][1]()
                pos[s] += 1
                if kind == "A":
                    return

        advance_to_a(0)
        turn = 0
        while pos[0] < len(todo[0]) or pos[1] < len(todo[1]):
            emit(turn, "B")
            advance_to_a(1 - turn)
            emit(turn, "C")
            turn = 1 - turn
